import numpy as np
import ml_dtypes

BF16 = ml_dtypes.bfloat16


def bf(x):
    return np.asarray(x, np.float32).astype(BF16)


def f32(x):
    return np.asarray(x, np.float32)


def f64(x):
    return np.asarray(x).astype(np.float64)


def striped(idx):
    return np.tile(idx.reshape(-1, 16).T, (8, 1))


D, S, M, N = 256, 4096, 128, 2048
SHARE, LO, SPAN = 0.7, 0.1, 0.3


def words(common, n):
    return f32((np.random.standard_normal((D, n)) + SHARE * common) * (LO + SPAN * np.random.random_sample((1, n))))


def unit(v):
    return v / np.sqrt(np.sum(v * v, axis=0, keepdims=True))


def setup_inputs():
    common = np.random.standard_normal((D, 1))
    return {"x": words(common, S), "cand": words(common, M), "offs": striped(np.random.permutation(np.tile(np.arange(S), 2))[:N])}


def reference(x, cand, offs):
    idx = offs[:16].T.reshape(-1)
    return unit(f64(cand)).T @ unit(f64(x)[:, idx])

@@ -1,0 +1,79 @@
+import concourse.mybir as mybir
+
+F32, BF16, U16 = mybir.dt.float32, mybir.dt.bfloat16, mybir.dt.uint16
+MULT = mybir.AluOpType.mult
+COPY = mybir.ActivationFunctionType.Copy
+ABS_RSQRT = mybir.ActivationFunctionType.Abs_reciprocal_sqrt
+
+P = 128
+FEATURES, WORDS, CANDS, PICKS = 256, 4096, 128, 2048
+BLOCKS = FEATURES // P
+PIECE = 512
+PIECES = PICKS // PIECE
+PIECE_OFFSET_COLUMNS = PIECE // 16
+LOAD_COLUMNS = WORDS // 2
+
+FLOPS = 2 * FEATURES * CANDS * PICKS
+
+
+def tile_knrmmodel_kernel(tc, x, cand, offs, out):
+    nc = tc.nc
+    with (
+        tc.tile_pool(name="held", bufs=1) as held,
+        tc.tile_pool(name="work", bufs=BLOCKS * PIECES) as work,
+        tc.tile_pool(name="results", bufs=PIECES) as results,
+        tc.psum_pool(name="dot_banks", bufs=PIECES) as dot_banks,
+        tc.psum_pool(name="sum_banks", bufs=PIECES) as sum_banks,
+    ):
+        offsets = held.tile([P, PICKS // 16], U16, name="offsets")
+        nc.sync.dma_start(offsets[:], offs)
+        cand_f32 = held.tile([P, BLOCKS, CANDS], F32, name="cand_f32")
+        nc.scalar.dma_start(cand_f32[:], cand.rearrange("(b p) m -> p b m", p=P))
+        tables = []
+        for b in range(BLOCKS):
+            table = held.tile([P, WORDS], F32, name=f"table{b}")
+            for first in range(0, WORDS, LOAD_COLUMNS):
+                nc.sync.dma_start(
+                    table[:, first : first + LOAD_COLUMNS],
+                    x[b * P : (b + 1) * P, first : first + LOAD_COLUMNS],
+                )
+            tables.append(table)
+
+        ones = held.tile([P, P], BF16, name="ones")
+        nc.vector.memset(ones[:], 1.0)
+
+        cand_squares = held.tile([P, BLOCKS, CANDS], BF16, name="cand_squares")
+        nc.vector.tensor_tensor(cand_squares[:], cand_f32[:], cand_f32[:], MULT)
+        cand_sums = sum_banks.tile([P, PIECE], F32, name="cand_sums", tag="sums")
+        for b in range(BLOCKS):
+            nc.tensor.matmul(
+                cand_sums[:, :CANDS], ones[:], cand_squares[:, b, :], start=(b == 0), stop=(b == BLOCKS - 1)
+            )
+        cand_rnorm = held.tile([P, CANDS], F32, name="cand_rnorm")
+        nc.scalar.activation(cand_rnorm[:], cand_sums[:, :CANDS], ABS_RSQRT)
+        cand_unit = held.tile([P, BLOCKS, CANDS], BF16, name="cand_unit")
+        for b in range(BLOCKS):
+            nc.vector.tensor_tensor(cand_unit[:, b, :], cand_f32[:, b, :], cand_rnorm[:], MULT)
+
+        dots = [dot_banks.tile([P, PIECE], F32, name=f"dots{q}", tag="dots") for q in range(PIECES)]
+        sums = [sum_banks.tile([P, PIECE], F32, name=f"sums{q}", tag="sums") for q in range(PIECES)]
+        for b in range(BLOCKS):
+            for q in range(PIECES):
+                piece_offsets = offsets[:, q * PIECE_OFFSET_COLUMNS : (q + 1) * PIECE_OFFSET_COLUMNS]
+                picked = work.tile([P, PIECE], F32, name="picked")
+                nc.scalar.activation(picked[:], tables[b][:].indirect(piece_offsets), COPY)
+                squares = work.tile([P, PIECE], BF16, name="squares")
+                nc.vector.tensor_tensor(squares[:], picked[:], picked[:], MULT)
+                rounded = work.tile([P, PIECE], BF16, name="rounded")
+                nc.vector.tensor_copy(rounded[:], picked[:])
+                nc.tensor.matmul(sums[q][:], ones[:], squares[:], start=(b == 0), stop=(b == BLOCKS - 1))
+                nc.tensor.matmul(
+                    dots[q][:], cand_unit[:, b, :], rounded[:], start=(b == 0), stop=(b == BLOCKS - 1)
+                )
+
+        for q in range(PIECES):
+            rnorm = results.tile([P, PIECE], F32, name="rnorm")
+            nc.scalar.activation(rnorm[:], sums[q][:], ABS_RSQRT)
+            cosine = results.tile([P, PIECE], F32, name="cosine")
+            nc.vector.tensor_tensor(cosine[:], dots[q][:], rnorm[:], MULT)
+            nc.sync.dma_start(out[:, q * PIECE : (q + 1) * PIECE], cosine[:])

@@ -11,7 +11,7 @@ BLOCKS = FEATURES // P
 PIECE = 512
 PIECES = PICKS // PIECE
 PIECE_OFFSET_COLUMNS = PIECE // 16
-LOAD_COLUMNS = WORDS // 2
+LOAD_COLUMNS = WORDS
 
 FLOPS = 2 * FEATURES * CANDS * PICKS
 

@@ -10,8 +10,7 @@ FEATURES, WORDS, CANDS, PICKS = 256, 4096, 128, 2048
 BLOCKS = FEATURES // P
 PIECE = 512
 PIECES = PICKS // PIECE
-PIECE_OFFSET_COLUMNS = PIECE // 16
-LOAD_COLUMNS = WORDS
+LOOKUP_PIECES = (2, 1)
 
 FLOPS = 2 * FEATURES * CANDS * PICKS
 
@@ -20,60 +19,78 @@ def tile_knrmmodel_kernel(tc, x, cand, offs, out):
     nc = tc.nc
     with (
         tc.tile_pool(name="held", bufs=1) as held,
-        tc.tile_pool(name="work", bufs=BLOCKS * PIECES) as work,
+        tc.tile_pool(name="work", bufs=PIECES) as work,
         tc.tile_pool(name="results", bufs=PIECES) as results,
         tc.psum_pool(name="dot_banks", bufs=PIECES) as dot_banks,
         tc.psum_pool(name="sum_banks", bufs=PIECES) as sum_banks,
     ):
         offsets = held.tile([P, PICKS // 16], U16, name="offsets")
         nc.sync.dma_start(offsets[:], offs)
-        cand_f32 = held.tile([P, BLOCKS, CANDS], F32, name="cand_f32")
-        nc.scalar.dma_start(cand_f32[:], cand.rearrange("(b p) m -> p b m", p=P))
         tables = []
         for b in range(BLOCKS):
             table = held.tile([P, WORDS], F32, name=f"table{b}")
-            for first in range(0, WORDS, LOAD_COLUMNS):
-                nc.sync.dma_start(
-                    table[:, first : first + LOAD_COLUMNS],
-                    x[b * P : (b + 1) * P, first : first + LOAD_COLUMNS],
-                )
+            nc.sync.dma_start(table[:], x[b * P : (b + 1) * P, :])
             tables.append(table)
+        cand_f32 = held.tile([P, BLOCKS, CANDS], F32, name="cand_f32")
+        nc.sync.dma_start(cand_f32[:], cand.rearrange("(b p) m -> p b m", p=P))
 
         ones = held.tile([P, P], BF16, name="ones")
         nc.vector.memset(ones[:], 1.0)
 
+        one = held.tile([P, 1], F32, name="one")
+        nc.vector.memset(one[:], 1.0)
+        warm = held.tile([P, 1], F32, name="warm")
+        nc.scalar.activation(warm[:], one[:], ABS_RSQRT)
+
+        def look_up(b, u):
+            width = LOOKUP_PIECES[b] * PIECE
+            lookup_offsets = offsets[:, u * width // 16 : (u + 1) * width // 16]
+            picked = work.tile([P, width], F32, name="picked", tag=f"picked{b}")
+            nc.scalar.activation(picked[:], tables[b][:].indirect(lookup_offsets), COPY)
+            squares = work.tile([P, width], BF16, name="squares", tag=f"squares{b}")
+            nc.vector.tensor_tensor(squares[:], picked[:], picked[:], MULT)
+            rounded = work.tile([P, width], BF16, name="rounded", tag=f"rounded{b}")
+            nc.vector.tensor_copy(rounded[:], picked[:])
+            return squares, rounded
+
+        def piece_of(tiles, b, q):
+            return tiles[q // LOOKUP_PIECES[b]][:, (q % LOOKUP_PIECES[b]) * PIECE : (q % LOOKUP_PIECES[b] + 1) * PIECE]
+
+        sums = [sum_banks.tile([P, PIECE], F32, name=f"sums{q}", tag="sums") for q in range(PIECES)]
+        rounded0 = []
+        for u in range(PIECES // LOOKUP_PIECES[0]):
+            squares, rounded = look_up(0, u)
+            rounded0.append(rounded)
+            for h in range(LOOKUP_PIECES[0]):
+                nc.tensor.matmul(
+                    sums[u * LOOKUP_PIECES[0] + h][:], ones[:], squares[:, h * PIECE : (h + 1) * PIECE],
+                    start=True, stop=False,
+                )
+
+        cand_bf16 = held.tile([P, BLOCKS, CANDS], BF16, name="cand_bf16")
+        nc.vector.tensor_copy(cand_bf16[:], cand_f32[:])
         cand_squares = held.tile([P, BLOCKS, CANDS], BF16, name="cand_squares")
         nc.vector.tensor_tensor(cand_squares[:], cand_f32[:], cand_f32[:], MULT)
-        cand_sums = sum_banks.tile([P, PIECE], F32, name="cand_sums", tag="sums")
+        cand_sums = dot_banks.tile([P, PIECE], F32, name="cand_sums", tag="dots")
         for b in range(BLOCKS):
             nc.tensor.matmul(
-                cand_sums[:, :CANDS], ones[:], cand_squares[:, b, :], start=(b == 0), stop=(b == BLOCKS - 1)
+                cand_sums[:, 0:1], cand_squares[:, b, :], ones[:, 0:1], start=(b == 0), stop=(b == BLOCKS - 1)
             )
-        cand_rnorm = held.tile([P, CANDS], F32, name="cand_rnorm")
-        nc.scalar.activation(cand_rnorm[:], cand_sums[:, :CANDS], ABS_RSQRT)
-        cand_unit = held.tile([P, BLOCKS, CANDS], BF16, name="cand_unit")
-        for b in range(BLOCKS):
-            nc.vector.tensor_tensor(cand_unit[:, b, :], cand_f32[:, b, :], cand_rnorm[:], MULT)
 
-        dots = [dot_banks.tile([P, PIECE], F32, name=f"dots{q}", tag="dots") for q in range(PIECES)]
-        sums = [sum_banks.tile([P, PIECE], F32, name=f"sums{q}", tag="sums") for q in range(PIECES)]
-        for b in range(BLOCKS):
-            for q in range(PIECES):
-                piece_offsets = offsets[:, q * PIECE_OFFSET_COLUMNS : (q + 1) * PIECE_OFFSET_COLUMNS]
-                picked = work.tile([P, PIECE], F32, name="picked")
-                nc.scalar.activation(picked[:], tables[b][:].indirect(piece_offsets), COPY)
-                squares = work.tile([P, PIECE], BF16, name="squares")
-                nc.vector.tensor_tensor(squares[:], picked[:], picked[:], MULT)
-                rounded = work.tile([P, PIECE], BF16, name="rounded")
-                nc.vector.tensor_copy(rounded[:], picked[:])
-                nc.tensor.matmul(sums[q][:], ones[:], squares[:], start=(b == 0), stop=(b == BLOCKS - 1))
-                nc.tensor.matmul(
-                    dots[q][:], cand_unit[:, b, :], rounded[:], start=(b == 0), stop=(b == BLOCKS - 1)
-                )
+        dots = []
+        for q in range(PIECES):
+            squares, rounded = look_up(1, q)
+            dots.append(dot_banks.tile([P, PIECE], F32, name=f"dots{q}", tag="dots"))
+            if q == PIECES - 1:
+                cand_rnorm = held.tile([P, 1], F32, name="cand_rnorm")
+                nc.scalar.activation(cand_rnorm[:], cand_sums[:, 0:1], ABS_RSQRT)
+            nc.tensor.matmul(dots[q][:], cand_bf16[:, 0, :], piece_of(rounded0, 0, q), start=True, stop=False)
+            nc.tensor.matmul(sums[q][:], ones[:], squares[:], start=False, stop=True)
+            nc.tensor.matmul(dots[q][:], cand_bf16[:, 1, :], rounded[:], start=False, stop=True)
 
         for q in range(PIECES):
             rnorm = results.tile([P, PIECE], F32, name="rnorm")
             nc.scalar.activation(rnorm[:], sums[q][:], ABS_RSQRT)
             cosine = results.tile([P, PIECE], F32, name="cosine")
-            nc.vector.tensor_tensor(cosine[:], dots[q][:], rnorm[:], MULT)
+            nc.vector.scalar_tensor_tensor(cosine[:], dots[q][:], cand_rnorm[:, 0:1], rnorm[:], MULT, MULT)
             nc.sync.dma_start(out[:, q * PIECE : (q + 1) * PIECE], cosine[:])

@@ -10,7 +10,7 @@ FEATURES, WORDS, CANDS, PICKS = 256, 4096, 128, 2048
 BLOCKS = FEATURES // P
 PIECE = 512
 PIECES = PICKS // PIECE
-LOOKUP_PIECES = (2, 1)
+LOOKUP_WIDTHS = ((1024, 1024), (512, 512, 512, 256, 256))
 
 FLOPS = 2 * FEATURES * CANDS * PICKS
 
@@ -42,30 +42,28 @@ def tile_knrmmodel_kernel(tc, x, cand, offs, out):
         warm = held.tile([P, 1], F32, name="warm")
         nc.scalar.activation(warm[:], one[:], ABS_RSQRT)
 
-        def look_up(b, u):
-            width = LOOKUP_PIECES[b] * PIECE
-            lookup_offsets = offsets[:, u * width // 16 : (u + 1) * width // 16]
-            picked = work.tile([P, width], F32, name="picked", tag=f"picked{b}")
-            nc.scalar.activation(picked[:], tables[b][:].indirect(lookup_offsets), COPY)
-            squares = work.tile([P, width], BF16, name="squares", tag=f"squares{b}")
+        def look_up(b, first, width):
+            picked = work.tile([P, width], F32, name="picked", tag=f"picked{width}")
+            nc.scalar.activation(
+                picked[:], tables[b][:].indirect(offsets[:, first // 16 : (first + width) // 16]), COPY
+            )
+            squares = work.tile([P, width], BF16, name="squares", tag=f"squares{width}")
             nc.vector.tensor_tensor(squares[:], picked[:], picked[:], MULT)
-            rounded = work.tile([P, width], BF16, name="rounded", tag=f"rounded{b}")
+            rounded = work.tile([P, width], BF16, name="rounded", tag=f"rounded{width}")
             nc.vector.tensor_copy(rounded[:], picked[:])
             return squares, rounded
 
-        def piece_of(tiles, b, q):
-            return tiles[q // LOOKUP_PIECES[b]][:, (q % LOOKUP_PIECES[b]) * PIECE : (q % LOOKUP_PIECES[b] + 1) * PIECE]
-
         sums = [sum_banks.tile([P, PIECE], F32, name=f"sums{q}", tag="sums") for q in range(PIECES)]
         rounded0 = []
-        for u in range(PIECES // LOOKUP_PIECES[0]):
-            squares, rounded = look_up(0, u)
-            rounded0.append(rounded)
-            for h in range(LOOKUP_PIECES[0]):
+        first = 0
+        for width in LOOKUP_WIDTHS[0]:
+            squares, rounded = look_up(0, first, width)
+            for at in range(0, width, PIECE):
                 nc.tensor.matmul(
-                    sums[u * LOOKUP_PIECES[0] + h][:], ones[:], squares[:, h * PIECE : (h + 1) * PIECE],
-                    start=True, stop=False,
+                    sums[(first + at) // PIECE][:], ones[:], squares[:, at : at + PIECE], start=True, stop=False
                 )
+                rounded0.append(rounded[:, at : at + PIECE])
+            first += width
 
         cand_bf16 = held.tile([P, BLOCKS, CANDS], BF16, name="cand_bf16")
         nc.vector.tensor_copy(cand_bf16[:], cand_f32[:])
@@ -76,17 +74,22 @@ def tile_knrmmodel_kernel(tc, x, cand, offs, out):
             nc.tensor.matmul(
                 cand_sums[:, 0:1], cand_squares[:, b, :], ones[:, 0:1], start=(b == 0), stop=(b == BLOCKS - 1)
             )
+        cand_rnorm = held.tile([P, 1], F32, name="cand_rnorm")
 
         dots = []
-        for q in range(PIECES):
-            squares, rounded = look_up(1, q)
-            dots.append(dot_banks.tile([P, PIECE], F32, name=f"dots{q}", tag="dots"))
-            if q == PIECES - 1:
-                cand_rnorm = held.tile([P, 1], F32, name="cand_rnorm")
-                nc.scalar.activation(cand_rnorm[:], cand_sums[:, 0:1], ABS_RSQRT)
-            nc.tensor.matmul(dots[q][:], cand_bf16[:, 0, :], piece_of(rounded0, 0, q), start=True, stop=False)
-            nc.tensor.matmul(sums[q][:], ones[:], squares[:], start=False, stop=True)
-            nc.tensor.matmul(dots[q][:], cand_bf16[:, 1, :], rounded[:], start=False, stop=True)
+        first = 0
+        for width in LOOKUP_WIDTHS[1]:
+            q, at = divmod(first, PIECE)
+            closes = at + width == PIECE
+            squares, rounded = look_up(1, first, width)
+            if at == 0:
+                if q == PIECES - 1:
+                    nc.scalar.activation(cand_rnorm[:], cand_sums[:, 0:1], ABS_RSQRT)
+                dots.append(dot_banks.tile([P, PIECE], F32, name=f"dots{q}", tag="dots"))
+                nc.tensor.matmul(dots[q][:], cand_bf16[:, 0, :], rounded0[q], start=True, stop=False)
+            nc.tensor.matmul(sums[q][:, at : at + width], ones[:], squares[:], start=False, stop=closes)
+            nc.tensor.matmul(dots[q][:, at : at + width], cand_bf16[:, 1, :], rounded[:], start=False, stop=closes)
+            first += width
 
         for q in range(PIECES):
             rnorm = results.tile([P, PIECE], F32, name="rnorm")

@@ -10,7 +10,7 @@ FEATURES, WORDS, CANDS, PICKS = 256, 4096, 128, 2048
 BLOCKS = FEATURES // P
 PIECE = 512
 PIECES = PICKS // PIECE
-LOOKUP_WIDTHS = ((1024, 1024), (512, 512, 512, 256, 256))
+LOOKUP_WIDTHS = ((1024, 1024), (512, 512, 512, 384, 128))
 
 FLOPS = 2 * FEATURES * CANDS * PICKS
 

@@ -10,7 +10,7 @@ FEATURES, WORDS, CANDS, PICKS = 256, 4096, 128, 2048
 BLOCKS = FEATURES // P
 PIECE = 512
 PIECES = PICKS // PIECE
-LOOKUP_WIDTHS = ((1024, 1024), (512, 512, 512, 384, 128))
+LOOKUP_WIDTHS = ((1024, 1024), (768, 576, 416, 288))
 
 FLOPS = 2 * FEATURES * CANDS * PICKS
 
@@ -53,16 +53,22 @@ def tile_knrmmodel_kernel(tc, x, cand, offs, out):
             nc.vector.tensor_copy(rounded[:], picked[:])
             return squares, rounded
 
+        def cut(first, width):
+            parts = []
+            for q in range(PIECES):
+                lo, hi = max(first, q * PIECE), min(first + width, (q + 1) * PIECE)
+                if lo < hi:
+                    parts.append((q, slice(lo - q * PIECE, hi - q * PIECE), slice(lo - first, hi - first)))
+            return parts
+
         sums = [sum_banks.tile([P, PIECE], F32, name=f"sums{q}", tag="sums") for q in range(PIECES)]
         rounded0 = []
         first = 0
         for width in LOOKUP_WIDTHS[0]:
             squares, rounded = look_up(0, first, width)
-            for at in range(0, width, PIECE):
-                nc.tensor.matmul(
-                    sums[(first + at) // PIECE][:], ones[:], squares[:, at : at + PIECE], start=True, stop=False
-                )
-                rounded0.append(rounded[:, at : at + PIECE])
+            for q, columns, found in cut(first, width):
+                nc.tensor.matmul(sums[q][:, columns], ones[:], squares[:, found], start=True, stop=False)
+                rounded0.append(rounded[:, found])
             first += width
 
         cand_bf16 = held.tile([P, BLOCKS, CANDS], BF16, name="cand_bf16")
@@ -79,16 +85,16 @@ def tile_knrmmodel_kernel(tc, x, cand, offs, out):
         dots = []
         first = 0
         for width in LOOKUP_WIDTHS[1]:
-            q, at = divmod(first, PIECE)
-            closes = at + width == PIECE
             squares, rounded = look_up(1, first, width)
-            if at == 0:
-                if q == PIECES - 1:
-                    nc.scalar.activation(cand_rnorm[:], cand_sums[:, 0:1], ABS_RSQRT)
-                dots.append(dot_banks.tile([P, PIECE], F32, name=f"dots{q}", tag="dots"))
-                nc.tensor.matmul(dots[q][:], cand_bf16[:, 0, :], rounded0[q], start=True, stop=False)
-            nc.tensor.matmul(sums[q][:, at : at + width], ones[:], squares[:], start=False, stop=closes)
-            nc.tensor.matmul(dots[q][:, at : at + width], cand_bf16[:, 1, :], rounded[:], start=False, stop=closes)
+            for q, columns, found in cut(first, width):
+                if q == len(dots):
+                    if q == PIECES - 1:
+                        nc.scalar.activation(cand_rnorm[:], cand_sums[:, 0:1], ABS_RSQRT)
+                    dots.append(dot_banks.tile([P, PIECE], F32, name=f"dots{q}", tag="dots"))
+                    nc.tensor.matmul(dots[q][:], cand_bf16[:, 0, :], rounded0[q], start=True, stop=False)
+                closes = columns.stop == PIECE
+                nc.tensor.matmul(sums[q][:, columns], ones[:], squares[:, found], start=False, stop=closes)
+                nc.tensor.matmul(dots[q][:, columns], cand_bf16[:, 1, :], rounded[:, found], start=False, stop=closes)
             first += width
 
         for q in range(PIECES):

@@ -19,6 +19,8 @@ def tile_knrmmodel_kernel(tc, x, cand, offs, out):
     nc = tc.nc
     with (
         tc.tile_pool(name="held", bufs=1) as held,
+        tc.tile_pool(name="picks", bufs=2) as picks,
+        tc.tile_pool(name="reused_picks", bufs=1) as reused_picks,
         tc.tile_pool(name="work", bufs=PIECES) as work,
         tc.tile_pool(name="results", bufs=PIECES) as results,
         tc.psum_pool(name="dot_banks", bufs=PIECES) as dot_banks,
@@ -42,8 +44,10 @@ def tile_knrmmodel_kernel(tc, x, cand, offs, out):
         warm = held.tile([P, 1], F32, name="warm")
         nc.scalar.activation(warm[:], one[:], ABS_RSQRT)
 
-        def look_up(b, first, width):
-            picked = work.tile([P, width], F32, name="picked", tag=f"picked{width}")
+        def look_up(b, i, first):
+            width = LOOKUP_WIDTHS[b][i]
+            pool = picks if i % 2 == 0 else reused_picks
+            picked = pool.tile([P, width], F32, name="picked", tag=f"picked{b}")
             nc.scalar.activation(
                 picked[:], tables[b][:].indirect(offsets[:, first // 16 : (first + width) // 16]), COPY
             )
@@ -64,8 +68,8 @@ def tile_knrmmodel_kernel(tc, x, cand, offs, out):
         sums = [sum_banks.tile([P, PIECE], F32, name=f"sums{q}", tag="sums") for q in range(PIECES)]
         rounded0 = []
         first = 0
-        for width in LOOKUP_WIDTHS[0]:
-            squares, rounded = look_up(0, first, width)
+        for i, width in enumerate(LOOKUP_WIDTHS[0]):
+            squares, rounded = look_up(0, i, first)
             for q, columns, found in cut(first, width):
                 nc.tensor.matmul(sums[q][:, columns], ones[:], squares[:, found], start=True, stop=False)
                 rounded0.append(rounded[:, found])
@@ -82,10 +86,19 @@ def tile_knrmmodel_kernel(tc, x, cand, offs, out):
             )
         cand_rnorm = held.tile([P, 1], F32, name="cand_rnorm")
 
+        def finish(q):
+            rnorm = results.tile([P, PIECE], F32, name="rnorm")
+            nc.scalar.activation(rnorm[:], sums[q][:], ABS_RSQRT)
+            cosine = results.tile([P, PIECE], F32, name="cosine")
+            nc.vector.scalar_tensor_tensor(cosine[:], dots[q][:], cand_rnorm[:, 0:1], rnorm[:], MULT, MULT)
+            nc.sync.dma_start(out[:, q * PIECE : (q + 1) * PIECE], cosine[:])
+
         dots = []
         first = 0
-        for width in LOOKUP_WIDTHS[1]:
-            squares, rounded = look_up(1, first, width)
+        for i, width in enumerate(LOOKUP_WIDTHS[1]):
+            if i == len(LOOKUP_WIDTHS[1]) - 1:
+                finish(0)
+            squares, rounded = look_up(1, i, first)
             for q, columns, found in cut(first, width):
                 if q == len(dots):
                     if q == PIECES - 1:
@@ -97,9 +110,5 @@ def tile_knrmmodel_kernel(tc, x, cand, offs, out):
                 nc.tensor.matmul(dots[q][:, columns], cand_bf16[:, 1, :], rounded[:, found], start=False, stop=closes)
             first += width
 
-        for q in range(PIECES):
-            rnorm = results.tile([P, PIECE], F32, name="rnorm")
-            nc.scalar.activation(rnorm[:], sums[q][:], ABS_RSQRT)
-            cosine = results.tile([P, PIECE], F32, name="cosine")
-            nc.vector.scalar_tensor_tensor(cosine[:], dots[q][:], cand_rnorm[:, 0:1], rnorm[:], MULT, MULT)
-            nc.sync.dma_start(out[:, q * PIECE : (q + 1) * PIECE], cosine[:])
+        for q in range(1, PIECES):
+            finish(q)

@@ -1,7 +1,7 @@
 import concourse.mybir as mybir
 
 F32, BF16, U16 = mybir.dt.float32, mybir.dt.bfloat16, mybir.dt.uint16
-MULT = mybir.AluOpType.mult
+MULT, POW = mybir.AluOpType.mult, mybir.AluOpType.pow
 COPY = mybir.ActivationFunctionType.Copy
 ABS_RSQRT = mybir.ActivationFunctionType.Abs_reciprocal_sqrt
 
@@ -19,8 +19,7 @@ def tile_knrmmodel_kernel(tc, x, cand, offs, out):
     nc = tc.nc
     with (
         tc.tile_pool(name="held", bufs=1) as held,
-        tc.tile_pool(name="picks", bufs=2) as picks,
-        tc.tile_pool(name="reused_picks", bufs=1) as reused_picks,
+        tc.tile_pool(name="handed_on", bufs=1) as handed_on,
         tc.tile_pool(name="work", bufs=PIECES) as work,
         tc.tile_pool(name="results", bufs=PIECES) as results,
         tc.psum_pool(name="dot_banks", bufs=PIECES) as dot_banks,
@@ -28,13 +27,12 @@ def tile_knrmmodel_kernel(tc, x, cand, offs, out):
     ):
         offsets = held.tile([P, PICKS // 16], U16, name="offsets")
         nc.sync.dma_start(offsets[:], offs)
-        tables = []
-        for b in range(BLOCKS):
-            table = held.tile([P, WORDS], F32, name=f"table{b}")
-            nc.sync.dma_start(table[:], x[b * P : (b + 1) * P, :])
-            tables.append(table)
+        x_blocks = x.rearrange("(p b) w -> b p w", b=BLOCKS)
+        tables = [held.tile([P, WORDS], F32, name=f"table{b}") for b in range(BLOCKS)]
+        nc.sync.dma_start(tables[0][:], x_blocks[0])
         cand_f32 = held.tile([P, BLOCKS, CANDS], F32, name="cand_f32")
-        nc.sync.dma_start(cand_f32[:], cand.rearrange("(b p) m -> p b m", p=P))
+        nc.sync.dma_start(cand_f32[:], cand.rearrange("(p b) m -> p b m", b=BLOCKS))
+        nc.sync.dma_start(tables[1][:], x_blocks[1])
 
         ones = held.tile([P, P], BF16, name="ones")
         nc.vector.memset(ones[:], 1.0)
@@ -44,16 +42,37 @@ def tile_knrmmodel_kernel(tc, x, cand, offs, out):
         warm = held.tile([P, 1], F32, name="warm")
         nc.scalar.activation(warm[:], one[:], ABS_RSQRT)
 
+        cand_bf16 = held.tile([P, BLOCKS, CANDS], BF16, name="cand_bf16")
+        nc.vector.tensor_copy(cand_bf16[:], cand_f32[:])
+        cand_squares = held.tile([P, BLOCKS, CANDS], BF16, name="cand_squares")
+        nc.vector.tensor_tensor(cand_squares[:], cand_f32[:], cand_f32[:], MULT)
+        cand_sums = dot_banks.tile([P, PIECE], F32, name="cand_sums", tag="dots")
+        for b in range(BLOCKS):
+            nc.tensor.matmul(
+                cand_sums[:, 0:1], cand_squares[:, b, :], ones[:, 0:1], start=(b == 0), stop=(b == BLOCKS - 1)
+            )
+        cand_norms2 = held.tile([P, 1], F32, name="cand_norms2")
+        nc.vector.tensor_copy(cand_norms2[:], cand_sums[:, 0:1])
+        minus_half = held.tile([P, 1], F32, name="minus_half")
+        nc.gpsimd.memset(minus_half[:], -0.5)
+        cand_rnorm = held.tile([P, 1], F32, name="cand_rnorm")
+        nc.gpsimd.tensor_tensor(cand_rnorm[:], cand_norms2[:], minus_half[:], POW)
+
         def look_up(b, i, first):
             width = LOOKUP_WIDTHS[b][i]
-            pool = picks if i % 2 == 0 else reused_picks
-            picked = pool.tile([P, width], F32, name="picked", tag=f"picked{b}")
+            hands_on = (b, i) == (1, 0)
+            takes_over = (b, i) == (1, len(LOOKUP_WIDTHS[1]) - 1)
+            picked = (handed_on if takes_over else work).tile(
+                [P, width], F32, name="picked", tag="handed_on" if takes_over else f"picked{width}"
+            )
             nc.scalar.activation(
                 picked[:], tables[b][:].indirect(offsets[:, first // 16 : (first + width) // 16]), COPY
             )
             squares = work.tile([P, width], BF16, name="squares", tag=f"squares{width}")
             nc.vector.tensor_tensor(squares[:], picked[:], picked[:], MULT)
-            rounded = work.tile([P, width], BF16, name="rounded", tag=f"rounded{width}")
+            rounded = (handed_on if hands_on else work).tile(
+                [P, width], BF16, name="rounded", tag="handed_on" if hands_on else f"rounded{width}"
+            )
             nc.vector.tensor_copy(rounded[:], picked[:])
             return squares, rounded
 
@@ -75,17 +94,6 @@ def tile_knrmmodel_kernel(tc, x, cand, offs, out):
                 rounded0.append(rounded[:, found])
             first += width
 
-        cand_bf16 = held.tile([P, BLOCKS, CANDS], BF16, name="cand_bf16")
-        nc.vector.tensor_copy(cand_bf16[:], cand_f32[:])
-        cand_squares = held.tile([P, BLOCKS, CANDS], BF16, name="cand_squares")
-        nc.vector.tensor_tensor(cand_squares[:], cand_f32[:], cand_f32[:], MULT)
-        cand_sums = dot_banks.tile([P, PIECE], F32, name="cand_sums", tag="dots")
-        for b in range(BLOCKS):
-            nc.tensor.matmul(
-                cand_sums[:, 0:1], cand_squares[:, b, :], ones[:, 0:1], start=(b == 0), stop=(b == BLOCKS - 1)
-            )
-        cand_rnorm = held.tile([P, 1], F32, name="cand_rnorm")
-
         def finish(q):
             rnorm = results.tile([P, PIECE], F32, name="rnorm")
             nc.scalar.activation(rnorm[:], sums[q][:], ABS_RSQRT)
@@ -101,8 +109,6 @@ def tile_knrmmodel_kernel(tc, x, cand, offs, out):
             squares, rounded = look_up(1, i, first)
             for q, columns, found in cut(first, width):
                 if q == len(dots):
-                    if q == PIECES - 1:
-                        nc.scalar.activation(cand_rnorm[:], cand_sums[:, 0:1], ABS_RSQRT)
                     dots.append(dot_banks.tile([P, PIECE], F32, name=f"dots{q}", tag="dots"))
                     nc.tensor.matmul(dots[q][:], cand_bf16[:, 0, :], rounded0[q], start=True, stop=False)
                 closes = columns.stop == PIECE

@@ -25,11 +25,11 @@ def tile_knrmmodel_kernel(tc, x, cand, offs, out):
         tc.psum_pool(name="dot_banks", bufs=PIECES) as dot_banks,
         tc.psum_pool(name="sum_banks", bufs=PIECES) as sum_banks,
     ):
-        offsets = held.tile([P, PICKS // 16], U16, name="offsets")
-        nc.sync.dma_start(offsets[:], offs)
         x_blocks = x.rearrange("(p b) w -> b p w", b=BLOCKS)
         tables = [held.tile([P, WORDS], F32, name=f"table{b}") for b in range(BLOCKS)]
         nc.sync.dma_start(tables[0][:], x_blocks[0])
+        offsets = held.tile([P, PICKS // 16], U16, name="offsets")
+        nc.sync.dma_start(offsets[:], offs)
         cand_f32 = held.tile([P, BLOCKS, CANDS], F32, name="cand_f32")
         nc.sync.dma_start(cand_f32[:], cand.rearrange("(p b) m -> p b m", b=BLOCKS))
         nc.sync.dma_start(tables[1][:], x_blocks[1])

@@ -1,7 +1,7 @@
 import concourse.mybir as mybir
 
 F32, BF16, U16 = mybir.dt.float32, mybir.dt.bfloat16, mybir.dt.uint16
-MULT, POW = mybir.AluOpType.mult, mybir.AluOpType.pow
+MULT = mybir.AluOpType.mult
 COPY = mybir.ActivationFunctionType.Copy
 ABS_RSQRT = mybir.ActivationFunctionType.Abs_reciprocal_sqrt
 
@@ -51,12 +51,7 @@ def tile_knrmmodel_kernel(tc, x, cand, offs, out):
             nc.tensor.matmul(
                 cand_sums[:, 0:1], cand_squares[:, b, :], ones[:, 0:1], start=(b == 0), stop=(b == BLOCKS - 1)
             )
-        cand_norms2 = held.tile([P, 1], F32, name="cand_norms2")
-        nc.vector.tensor_copy(cand_norms2[:], cand_sums[:, 0:1])
-        minus_half = held.tile([P, 1], F32, name="minus_half")
-        nc.gpsimd.memset(minus_half[:], -0.5)
         cand_rnorm = held.tile([P, 1], F32, name="cand_rnorm")
-        nc.gpsimd.tensor_tensor(cand_rnorm[:], cand_norms2[:], minus_half[:], POW)
 
         def look_up(b, i, first):
             width = LOOKUP_WIDTHS[b][i]
@@ -93,6 +88,8 @@ def tile_knrmmodel_kernel(tc, x, cand, offs, out):
                 nc.tensor.matmul(sums[q][:, columns], ones[:], squares[:, found], start=True, stop=False)
                 rounded0.append(rounded[:, found])
             first += width
+
+        nc.scalar.activation(cand_rnorm[:], cand_sums[:, 0:1], ABS_RSQRT)
 
         def finish(q):
             rnorm = results.tile([P, PIECE], F32, name="rnorm")

import concourse.mybir as mybir

F32, BF16, U16 = mybir.dt.float32, mybir.dt.bfloat16, mybir.dt.uint16
MULT = mybir.AluOpType.mult
COPY = mybir.ActivationFunctionType.Copy
ABS_RSQRT = mybir.ActivationFunctionType.Abs_reciprocal_sqrt

P = 128
FEATURES, WORDS, CANDS, PICKS = 256, 4096, 128, 2048
BLOCKS = FEATURES // P
PIECE = 512
PIECES = PICKS // PIECE
LOOKUP_WIDTHS = ((1024, 1024), (768, 576, 416, 288))

FLOPS = 2 * FEATURES * CANDS * PICKS


def tile_knrmmodel_kernel(tc, x, cand, offs, out):
    nc = tc.nc
    with (
        tc.tile_pool(name="held", bufs=1) as held,
        tc.tile_pool(name="handed_on", bufs=1) as handed_on,
        tc.tile_pool(name="work", bufs=PIECES) as work,
        tc.tile_pool(name="results", bufs=PIECES) as results,
        tc.psum_pool(name="dot_banks", bufs=PIECES) as dot_banks,
        tc.psum_pool(name="sum_banks", bufs=PIECES) as sum_banks,
    ):
        x_blocks = x.rearrange("(p b) w -> b p w", b=BLOCKS)
        tables = [held.tile([P, WORDS], F32, name=f"table{b}") for b in range(BLOCKS)]
        nc.sync.dma_start(tables[0][:], x_blocks[0])
        offsets = held.tile([P, PICKS // 16], U16, name="offsets")
        nc.sync.dma_start(offsets[:], offs)
        cand_f32 = held.tile([P, BLOCKS, CANDS], F32, name="cand_f32")
        nc.sync.dma_start(cand_f32[:], cand.rearrange("(p b) m -> p b m", b=BLOCKS))
        nc.sync.dma_start(tables[1][:], x_blocks[1])

        ones = held.tile([P, P], BF16, name="ones")
        nc.vector.memset(ones[:], 1.0)

        one = held.tile([P, 1], F32, name="one")
        nc.vector.memset(one[:], 1.0)
        warm = held.tile([P, 1], F32, name="warm")
        nc.scalar.activation(warm[:], one[:], ABS_RSQRT)

        cand_bf16 = held.tile([P, BLOCKS, CANDS], BF16, name="cand_bf16")
        nc.vector.tensor_copy(cand_bf16[:], cand_f32[:])
        cand_squares = held.tile([P, BLOCKS, CANDS], BF16, name="cand_squares")
        nc.vector.tensor_tensor(cand_squares[:], cand_f32[:], cand_f32[:], MULT)
        cand_sums = dot_banks.tile([P, PIECE], F32, name="cand_sums", tag="dots")
        for b in range(BLOCKS):
            nc.tensor.matmul(
                cand_sums[:, 0:1], cand_squares[:, b, :], ones[:, 0:1], start=(b == 0), stop=(b == BLOCKS - 1)
            )
        cand_rnorm = held.tile([P, 1], F32, name="cand_rnorm")

        def look_up(b, i, first):
            width = LOOKUP_WIDTHS[b][i]
            hands_on = (b, i) == (1, 0)
            takes_over = (b, i) == (1, len(LOOKUP_WIDTHS[1]) - 1)
            picked = (handed_on if takes_over else work).tile(
                [P, width], F32, name="picked", tag="handed_on" if takes_over else f"picked{width}"
            )
            nc.scalar.activation(
                picked[:], tables[b][:].indirect(offsets[:, first // 16 : (first + width) // 16]), COPY
            )
            squares = work.tile([P, width], BF16, name="squares", tag=f"squares{width}")
            nc.vector.tensor_tensor(squares[:], picked[:], picked[:], MULT)
            rounded = (handed_on if hands_on else work).tile(
                [P, width], BF16, name="rounded", tag="handed_on" if hands_on else f"rounded{width}"
            )
            nc.vector.tensor_copy(rounded[:], picked[:])
            return squares, rounded

        def cut(first, width):
            parts = []
            for q in range(PIECES):
                lo, hi = max(first, q * PIECE), min(first + width, (q + 1) * PIECE)
                if lo < hi:
                    parts.append((q, slice(lo - q * PIECE, hi - q * PIECE), slice(lo - first, hi - first)))
            return parts

        sums = [sum_banks.tile([P, PIECE], F32, name=f"sums{q}", tag="sums") for q in range(PIECES)]
        rounded0 = []
        first = 0
        for i, width in enumerate(LOOKUP_WIDTHS[0]):
            squares, rounded = look_up(0, i, first)
            for q, columns, found in cut(first, width):
                nc.tensor.matmul(sums[q][:, columns], ones[:], squares[:, found], start=True, stop=False)
                rounded0.append(rounded[:, found])
            first += width

        nc.scalar.activation(cand_rnorm[:], cand_sums[:, 0:1], ABS_RSQRT)

        def finish(q):
            rnorm = results.tile([P, PIECE], F32, name="rnorm")
            nc.scalar.activation(rnorm[:], sums[q][:], ABS_RSQRT)
            cosine = results.tile([P, PIECE], F32, name="cosine")
            nc.vector.scalar_tensor_tensor(cosine[:], dots[q][:], cand_rnorm[:, 0:1], rnorm[:], MULT, MULT)
            nc.sync.dma_start(out[:, q * PIECE : (q + 1) * PIECE], cosine[:])

        dots = []
        first = 0
        for i, width in enumerate(LOOKUP_WIDTHS[1]):
            if i == len(LOOKUP_WIDTHS[1]) - 1:
                finish(0)
            squares, rounded = look_up(1, i, first)
            for q, columns, found in cut(first, width):
                if q == len(dots):
                    dots.append(dot_banks.tile([P, PIECE], F32, name=f"dots{q}", tag="dots"))
                    nc.tensor.matmul(dots[q][:], cand_bf16[:, 0, :], rounded0[q], start=True, stop=False)
                closes = columns.stop == PIECE
                nc.tensor.matmul(sums[q][:, columns], ones[:], squares[:, found], start=False, stop=closes)
                nc.tensor.matmul(dots[q][:, columns], cand_bf16[:, 1, :], rounded[:, found], start=False, stop=closes)
            first += width

        for q in range(1, PIECES):
            finish(q)
